import numpy as np
import ml_dtypes


def mxq(x, axis, fmt="e4m3"):
    dtype, down = {"e4m3": (ml_dtypes.float8_e4m3fn, 7), "e5m2": (ml_dtypes.float8_e5m2, 14)}[fmt]
    v = np.moveaxis(np.asarray(x, np.float32).astype(ml_dtypes.bfloat16).astype(np.float64), axis, -1)
    blocks = v.reshape(v.shape[:-1] + (-1, 32))
    amax = np.abs(blocks).max(-1, keepdims=True)
    byte = np.maximum(np.where(amax > 0, np.frexp(amax)[1] - 1 + 127, 0) - down, 1)
    scale = np.exp2(byte - 127.0)
    codes = (blocks / scale).astype(np.float32).astype(dtype).astype(np.float64)
    return np.moveaxis((codes * scale).reshape(v.shape), -1, axis)


WIDE = False


def mx_kscale(k):
    if not WIDE:
        return np.ones(k)
    levels = np.array([10, -10, 5, -5, 0])
    a = np.random.permutation(np.resize(levels, k // 512 * 4)).reshape(k // 512, 4)
    idx = np.arange(k)
    return np.exp2(a[idx // 512, idx % 128 // 32])


BF16 = ml_dtypes.bfloat16


def bf(x):
    return np.asarray(x, np.float32).astype(BF16)


def f64(x):
    return np.asarray(x).astype(np.float64)


B, S, D, H, F, QB = 1, 1024, 1024, 8, 1536, 512
HD = D // H
EPS = 1e-5


def setup_inputs():
    s = mx_kscale(D)
    return {"x": bf(np.random.standard_normal((B, S, D))),
            "rms_w": bf((1.0 + 0.1 * np.random.standard_normal(D)) * s),
            "w_qkv": bf(np.random.standard_normal((3 * D, D)) * 1.5 / np.sqrt(D) / s[None, :])}


def reference(x, rms_w, w_qkv):
    xf = f64(x)
    xn = xf / np.sqrt(np.mean(xf * xf, axis=-1, keepdims=True) + EPS) * f64(rms_w)
    y = mxq(xn, 2, "e4m3") @ mxq(f64(w_qkv), 1, "e4m3").T
    return y.reshape(B, S, 3, H, HD).transpose(2, 0, 3, 1, 4)

@@ -1,0 +1,266 @@
+from contextlib import ExitStack
+
+import concourse.mybir as mybir
+from concourse.masks import make_identity
+
+F32 = mybir.dt.float32
+BF16 = mybir.dt.bfloat16
+U32 = mybir.dt.uint32
+U8 = mybir.dt.uint8
+FP8X4 = mybir.dt.float8_e4m3fn_x4
+ACT = mybir.ActivationFunctionType
+ALU = mybir.AluOpType
+
+P = 128
+S = 1024
+D = 1024
+N_OUT = 3072
+EPS = 1e-5
+PACK = 4
+K_PASS = P * PACK
+PASSES = D // K_PASS
+HALVES = 2
+S_TILES = S // P
+N_ROUND = 512
+ROUNDS = N_OUT // N_ROUND
+HEAD = 128
+HEADS_PER_ROUND = N_ROUND // HEAD
+ROW_PAIR = 2
+GROUP_ROWS = P * ROW_PAIR
+GROUPS_PER_ROUND = N_ROUND // GROUP_ROWS
+W_BANKS = PASSES * GROUPS_PER_ROUND
+LEAD = 4
+NEXT_W_SLOT = 2
+STORE_TILES = 4
+
+FLOPS = 2 * S * D * N_OUT
+
+
+def tile_transformerblock_pa_kernel(tc, x, rms_w, w_qkv, out):
+    nc = tc.nc
+    x_rows = x.rearrange("b (p m) d -> p (b m) d", m=S_TILES)
+    out_rows = out.rearrange("c b h (p m) f -> p (c b h) m f", m=S_TILES)
+    w_rows = w_qkv.rearrange("(r q a) d -> q r a d", q=P, a=ROW_PAIR)
+
+    with ExitStack() as ctx:
+        keep = ctx.enter_context(tc.tile_pool(name="keep", bufs=1))
+        scratch = ctx.enter_context(tc.tile_pool(name="scratch", bufs=2))
+        x_group_pool = ctx.enter_context(tc.tile_pool(name="x_group", bufs=3))
+        w_group_pool = ctx.enter_context(tc.tile_pool(name="w_group", bufs=2))
+        stage_pool = ctx.enter_context(tc.tile_pool(name="stage", bufs=24 // STORE_TILES))
+        psum_tr = ctx.enter_context(tc.psum_pool(name="psum_tr", bufs=4))
+        psum_acc = ctx.enter_context(tc.psum_pool(name="psum_acc", bufs=4))
+
+        x_sb = keep.tile([P, S_TILES, D], BF16)
+        xn = keep.tile([P, S_TILES, D], BF16)
+        w_sb = keep.tile([P, ROUNDS * GROUPS_PER_ROUND, ROW_PAIR, D], BF16)
+        gain_rows = keep.tile([P, D], BF16)
+        gain_bc = keep.tile([P, D], BF16)
+        ones = keep.tile([P, P], BF16)
+        ident = keep.tile([P, P], F32)
+        eps_col = keep.tile([P, 1], F32)
+        warm = keep.tile([P, 1], F32)
+        sum_sq = keep.tile([P, S_TILES], F32)
+        rms = keep.tile([P, S_TILES], F32)
+        inv_rms = keep.tile([P, S_TILES], F32)
+        x_codes = keep.tile([P, S_TILES, PASSES * P], U32, align_bytes=64)
+        x_scales = keep.tile([P, S_TILES, PASSES * P], U8, align_bytes=64)
+        w_codes = keep.tile([P, ROUNDS, PASSES * N_ROUND], U32, align_bytes=64)
+        w_scales = keep.tile([P, ROUNDS, PASSES * N_ROUND], U8, align_bytes=64)
+
+        x_banks = {}
+        x_grouped = {}
+        w_banks = {}
+        w_grouped = {}
+        acc_banks = {}
+        stages = {}
+
+        def leave_psum(index, dst, src):
+            if index % 2 == 0:
+                nc.scalar.copy(out=dst, in_=src)
+            else:
+                nc.vector.tensor_copy(out=dst, in_=src)
+
+        def load_x(first):
+            tiles = slice(first, first + 2)
+            nc.sync.dma_start(out=x_sb[:, tiles, :], in_=x_rows[:, tiles, :])
+
+        def load_w(j):
+            groups = slice(GROUPS_PER_ROUND * j, GROUPS_PER_ROUND * (j + 1))
+            nc.sync.dma_start(out=w_sb[:, groups, :, :], in_=w_rows[:, groups, :, :])
+
+        def x_stats(m):
+            squares = scratch.tile([P, D], BF16)
+            nc.scalar.activation(
+                out=squares[:], in_=x_sb[:, m, :], func=ACT.Square, accum_out=sum_sq[:, m : m + 1]
+            )
+            nc.scalar.activation(
+                out=rms[:, m : m + 1],
+                in_=sum_sq[:, m : m + 1],
+                func=ACT.Sqrt,
+                bias=eps_col[:, 0:1],
+                scale=1.0 / D,
+            )
+
+        def x_scale(m):
+            nc.vector.reciprocal(out=inv_rms[:, m : m + 1], in_=rms[:, m : m + 1])
+            nc.vector.scalar_tensor_tensor(
+                out=xn[:, m, :],
+                in0=x_sb[:, m, :],
+                scalar=inv_rms[:, m : m + 1],
+                in1=gain_bc[:],
+                op0=ALU.mult,
+                op1=ALU.mult,
+            )
+
+        def x_transpose(m):
+            bank = psum_tr.tile([P, PASSES, HALVES, P], F32, tag="tr")
+            words = xn[:, m, :].bitcast(F32)
+            for g in range(PASSES):
+                for u in range(HALVES):
+                    first = (HALVES * g + u) * P
+                    nc.tensor.transpose(bank[:, g, u, :], words[:, first : first + P], ident[:])
+            x_banks[m] = bank
+
+        def x_regroup(m):
+            grouped = x_group_pool.tile([P, PASSES * P * PACK], BF16, align_bytes=64)
+            nc.scalar.copy(
+                out=grouped[:].bitcast(F32).rearrange("p (g s u) -> p g s u", g=PASSES, u=HALVES),
+                in_=x_banks[m][:].rearrange("p g u s -> p g s u"),
+            )
+            x_grouped[m] = grouped
+
+        def x_quantise(m):
+            nc.vector.quantize_mx(
+                out=x_codes[:, m, :].bitcast(FP8X4), scales=x_scales[:, m, :], in_=x_grouped[m][:]
+            )
+
+        def x_step(step):
+            if 0 <= step - 3 < S_TILES:
+                x_quantise(step - 3)
+            if 0 <= step - 2 < S_TILES:
+                x_regroup(step - 2)
+            if 0 <= step - 1 < S_TILES:
+                x_scale(step - 1)
+                x_transpose(step - 1)
+            if step < S_TILES:
+                x_stats(step)
+
+        def w_transpose(j):
+            banks = []
+            for g in range(PASSES):
+                for r in range(GROUPS_PER_ROUND):
+                    bank = psum_tr.tile([P, ROW_PAIR, HALVES, P], F32, tag="tr")
+                    for a in range(ROW_PAIR):
+                        words = w_sb[:, GROUPS_PER_ROUND * j + r, a, :].bitcast(F32)
+                        for u in range(HALVES):
+                            first = (HALVES * g + u) * P
+                            nc.tensor.transpose(
+                                bank[:, a, u, :], words[:, first : first + P], ident[:]
+                            )
+                    banks.append(bank)
+            w_banks[j] = banks
+            grouped = w_group_pool.tile([P, PASSES * N_ROUND * PACK], BF16, align_bytes=64)
+            w_grouped[j] = grouped
+
+        def w_regroup(j, b):
+            leave_psum(
+                b,
+                w_grouped[j][:]
+                .bitcast(F32)
+                .rearrange("p (b q a u) -> p b q a u", b=W_BANKS, a=ROW_PAIR, u=HALVES)[:, b],
+                w_banks[j][b][:].rearrange("p a u q -> p q a u"),
+            )
+
+        def w_quantise(j, g):
+            cols = slice(g * N_ROUND, (g + 1) * N_ROUND)
+            nc.vector.quantize_mx(
+                out=w_codes[:, j, cols].bitcast(FP8X4),
+                scales=w_scales[:, j, cols],
+                in_=w_grouped[j][:, g * N_ROUND * PACK : (g + 1) * N_ROUND * PACK],
+            )
+
+        def product(j, m):
+            acc = psum_acc.tile([P, N_ROUND], F32, tag="acc")
+            for g in range(PASSES):
+                nc.tensor.matmul_mx(
+                    out=acc[:],
+                    lhsT=x_codes[:, m, g * P : (g + 1) * P].bitcast(FP8X4),
+                    lhsT_scale=x_scales[:, m, g * P : (g + 1) * P],
+                    rhs=w_codes[:, j, g * N_ROUND : (g + 1) * N_ROUND].bitcast(FP8X4),
+                    rhs_scale=w_scales[:, j, g * N_ROUND : (g + 1) * N_ROUND],
+                    start=(g == 0),
+                    stop=(g == PASSES - 1),
+                )
+            acc_banks[m] = acc
+
+        def collect(j, m):
+            if m % STORE_TILES == 0:
+                stage = stage_pool.tile([P, HEADS_PER_ROUND, STORE_TILES, HEAD], F32)
+                stages[0] = stage
+            leave_psum(
+                m,
+                stages[0][:, :, m % STORE_TILES, :],
+                acc_banks[m][:].rearrange("p (h f) -> p h f", h=HEADS_PER_ROUND),
+            )
+            if m % STORE_TILES == STORE_TILES - 1:
+                nc.sync.dma_start(
+                    out=out_rows[
+                        :,
+                        HEADS_PER_ROUND * j : HEADS_PER_ROUND * (j + 1),
+                        m + 1 - STORE_TILES : m + 1,
+                        :,
+                    ],
+                    in_=stages[0][:],
+                )
+
+        nc.vector.memset(gain_rows[:], 0.0)
+        nc.sync.dma_start(out=gain_rows[0:1, :], in_=rms_w.unsqueeze(0))
+        load_x(0)
+        load_x(2)
+        load_w(0)
+        load_x(4)
+        load_x(6)
+        for j in range(1, ROUNDS):
+            load_w(j)
+
+        nc.vector.memset(eps_col[:], EPS)
+        nc.vector.memset(ones[:], 1.0)
+        make_identity(nc, ident[:])
+        nc.scalar.activation(out=warm[:], in_=eps_col[:], func=ACT.Sqrt)
+
+        for half in range(D // N_ROUND):
+            cols = slice(half * N_ROUND, (half + 1) * N_ROUND)
+            spread = psum_tr.tile([P, N_ROUND], F32, tag="tr")
+            nc.tensor.matmul(out=spread[:], lhsT=ones[:], rhs=gain_rows[:, cols], start=True, stop=True)
+            nc.vector.tensor_copy(out=gain_bc[:, cols], in_=spread[:])
+
+        x_step(0)
+        x_step(1)
+        x_step(2)
+        w_transpose(0)
+        w_regroup(0, 0)
+        w_regroup(0, 1)
+        x_step(3)
+        w_regroup(0, 2)
+        w_regroup(0, 3)
+        w_quantise(0, 0)
+        w_quantise(0, 1)
+
+        for j in range(ROUNDS):
+            for m in range(S_TILES):
+                product(j, m)
+                b = m - NEXT_W_SLOT
+                if j + 1 < ROUNDS:
+                    if b == 0:
+                        w_transpose(j + 1)
+                    if 0 <= b < W_BANKS:
+                        w_regroup(j + 1, b)
+                collect(j, m)
+                if j + 1 < ROUNDS:
+                    if b == 2:
+                        w_quantise(j + 1, 0)
+                    if b == 4:
+                        w_quantise(j + 1, 1)
+                if j == 0:
+                    x_step(m + LEAD)

@@ -50,6 +50,7 @@ def tile_transformerblock_pa_kernel(tc, x, rms_w, w_qkv, out):
         stage_pool = ctx.enter_context(tc.tile_pool(name="stage", bufs=24 // STORE_TILES))
         psum_tr = ctx.enter_context(tc.psum_pool(name="psum_tr", bufs=4))
         psum_acc = ctx.enter_context(tc.psum_pool(name="psum_acc", bufs=4))
+        ctx.enter_context(tc.manual_schedule())
 
         x_sb = keep.tile([P, S_TILES, D], BF16)
         xn = keep.tile([P, S_TILES, D], BF16)

@@ -29,9 +29,7 @@ ROW_PAIR = 2
 GROUP_ROWS = P * ROW_PAIR
 GROUPS_PER_ROUND = N_ROUND // GROUP_ROWS
 W_BANKS = PASSES * GROUPS_PER_ROUND
-LEAD = 4
-NEXT_W_SLOT = 2
-STORE_TILES = 4
+GROUP_TILES = 4
 
 FLOPS = 2 * S * D * N_OUT
 
@@ -47,10 +45,9 @@ def tile_transformerblock_pa_kernel(tc, x, rms_w, w_qkv, out):
         scratch = ctx.enter_context(tc.tile_pool(name="scratch", bufs=2))
         x_group_pool = ctx.enter_context(tc.tile_pool(name="x_group", bufs=3))
         w_group_pool = ctx.enter_context(tc.tile_pool(name="w_group", bufs=2))
-        stage_pool = ctx.enter_context(tc.tile_pool(name="stage", bufs=24 // STORE_TILES))
+        stage_pool = ctx.enter_context(tc.tile_pool(name="stage", bufs=24 // GROUP_TILES))
         psum_tr = ctx.enter_context(tc.psum_pool(name="psum_tr", bufs=4))
         psum_acc = ctx.enter_context(tc.psum_pool(name="psum_acc", bufs=4))
-        ctx.enter_context(tc.manual_schedule())
 
         x_sb = keep.tile([P, S_TILES, D], BF16)
         xn = keep.tile([P, S_TILES, D], BF16)
@@ -136,16 +133,19 @@ def tile_transformerblock_pa_kernel(tc, x, rms_w, w_qkv, out):
                 out=x_codes[:, m, :].bitcast(FP8X4), scales=x_scales[:, m, :], in_=x_grouped[m][:]
             )
 
-        def x_step(step):
-            if 0 <= step - 3 < S_TILES:
-                x_quantise(step - 3)
-            if 0 <= step - 2 < S_TILES:
-                x_regroup(step - 2)
-            if 0 <= step - 1 < S_TILES:
-                x_scale(step - 1)
-                x_transpose(step - 1)
-            if step < S_TILES:
-                x_stats(step)
+        def x_prepare(m):
+            x_stats(m)
+            x_scale(m)
+            x_transpose(m)
+            x_regroup(m)
+            x_quantise(m)
+
+        def w_prepare(j):
+            w_transpose(j)
+            for b in range(W_BANKS):
+                w_regroup(j, b)
+            for g in range(PASSES):
+                w_quantise(j, g)
 
         def w_transpose(j):
             banks = []
@@ -196,20 +196,20 @@ def tile_transformerblock_pa_kernel(tc, x, rms_w, w_qkv, out):
             acc_banks[m] = acc
 
         def collect(j, m):
-            if m % STORE_TILES == 0:
-                stage = stage_pool.tile([P, HEADS_PER_ROUND, STORE_TILES, HEAD], F32)
+            if m % GROUP_TILES == 0:
+                stage = stage_pool.tile([P, HEADS_PER_ROUND, GROUP_TILES, HEAD], F32)
                 stages[0] = stage
             leave_psum(
                 m,
-                stages[0][:, :, m % STORE_TILES, :],
+                stages[0][:, :, m % GROUP_TILES, :],
                 acc_banks[m][:].rearrange("p (h f) -> p h f", h=HEADS_PER_ROUND),
             )
-            if m % STORE_TILES == STORE_TILES - 1:
+            if m % GROUP_TILES == GROUP_TILES - 1:
                 nc.sync.dma_start(
                     out=out_rows[
                         :,
                         HEADS_PER_ROUND * j : HEADS_PER_ROUND * (j + 1),
-                        m + 1 - STORE_TILES : m + 1,
+                        m + 1 - GROUP_TILES : m + 1,
                         :,
                     ],
                     in_=stages[0][:],
@@ -236,32 +236,18 @@ def tile_transformerblock_pa_kernel(tc, x, rms_w, w_qkv, out):
             nc.tensor.matmul(out=spread[:], lhsT=ones[:], rhs=gain_rows[:, cols], start=True, stop=True)
             nc.vector.tensor_copy(out=gain_bc[:, cols], in_=spread[:])
 
-        x_step(0)
-        x_step(1)
-        x_step(2)
-        w_transpose(0)
-        w_regroup(0, 0)
-        w_regroup(0, 1)
-        x_step(3)
-        w_regroup(0, 2)
-        w_regroup(0, 3)
-        w_quantise(0, 0)
-        w_quantise(0, 1)
+        x_prepare(0)
+        x_prepare(1)
+        w_prepare(0)
+        for m in range(2, GROUP_TILES):
+            x_prepare(m)
 
-        for j in range(ROUNDS):
-            for m in range(S_TILES):
-                product(j, m)
-                b = m - NEXT_W_SLOT
-                if j + 1 < ROUNDS:
-                    if b == 0:
-                        w_transpose(j + 1)
-                    if 0 <= b < W_BANKS:
-                        w_regroup(j + 1, b)
-                collect(j, m)
-                if j + 1 < ROUNDS:
-                    if b == 2:
-                        w_quantise(j + 1, 0)
-                    if b == 4:
-                        w_quantise(j + 1, 1)
-                if j == 0:
-                    x_step(m + LEAD)
+        for group in range(S_TILES // GROUP_TILES):
+            for j in range(ROUNDS):
+                if group == 0 and j + 1 < ROUNDS:
+                    w_prepare(j + 1)
+                for m in range(group * GROUP_TILES, (group + 1) * GROUP_TILES):
+                    product(j, m)
+                    collect(j, m)
+                if j < GROUP_TILES and group + 1 < S_TILES // GROUP_TILES:
+                    x_prepare((group + 1) * GROUP_TILES + j)

@@ -166,7 +166,7 @@ def tile_transformerblock_pa_kernel(tc, x, rms_w, w_qkv, out):
 
         def w_regroup(j, b):
             leave_psum(
-                b,
+                0 if b < W_BANKS - 1 else 1,
                 w_grouped[j][:]
                 .bitcast(F32)
                 .rearrange("p (b q a u) -> p b q a u", b=W_BANKS, a=ROW_PAIR, u=HALVES)[:, b],

@@ -166,7 +166,7 @@ def tile_transformerblock_pa_kernel(tc, x, rms_w, w_qkv, out):
 
         def w_regroup(j, b):
             leave_psum(
-                0 if b < W_BANKS - 1 else 1,
+                0,
                 w_grouped[j][:]
                 .bitcast(F32)
                 .rearrange("p (b q a u) -> p b q a u", b=W_BANKS, a=ROW_PAIR, u=HALVES)[:, b],
@@ -200,7 +200,7 @@ def tile_transformerblock_pa_kernel(tc, x, rms_w, w_qkv, out):
                 stage = stage_pool.tile([P, HEADS_PER_ROUND, GROUP_TILES, HEAD], F32)
                 stages[0] = stage
             leave_psum(
-                m,
+                m if m >= GROUP_TILES else min(m, 1),
                 stages[0][:, :, m % GROUP_TILES, :],
                 acc_banks[m][:].rearrange("p (h f) -> p h f", h=HEADS_PER_ROUND),
             )

@@ -38,7 +38,7 @@ def tile_transformerblock_pa_kernel(tc, x, rms_w, w_qkv, out):
     nc = tc.nc
     x_rows = x.rearrange("b (p m) d -> p (b m) d", m=S_TILES)
     out_rows = out.rearrange("c b h (p m) f -> p (c b h) m f", m=S_TILES)
-    w_rows = w_qkv.rearrange("(r q a) d -> q r a d", q=P, a=ROW_PAIR)
+    w_rows = w_qkv.rearrange("(j q r a) d -> q j r a d", q=P, r=GROUPS_PER_ROUND, a=ROW_PAIR)
 
     with ExitStack() as ctx:
         keep = ctx.enter_context(tc.tile_pool(name="keep", bufs=1))
@@ -51,7 +51,7 @@ def tile_transformerblock_pa_kernel(tc, x, rms_w, w_qkv, out):
 
         x_sb = keep.tile([P, S_TILES, D], BF16)
         xn = keep.tile([P, S_TILES, D], BF16)
-        w_sb = keep.tile([P, ROUNDS * GROUPS_PER_ROUND, ROW_PAIR, D], BF16)
+        w_sb = keep.tile([P, ROUNDS, GROUPS_PER_ROUND, ROW_PAIR, D], BF16)
         gain_rows = keep.tile([P, D], BF16)
         gain_bc = keep.tile([P, D], BF16)
         ones = keep.tile([P, P], BF16)
@@ -84,8 +84,7 @@ def tile_transformerblock_pa_kernel(tc, x, rms_w, w_qkv, out):
             nc.sync.dma_start(out=x_sb[:, tiles, :], in_=x_rows[:, tiles, :])
 
         def load_w(j):
-            groups = slice(GROUPS_PER_ROUND * j, GROUPS_PER_ROUND * (j + 1))
-            nc.sync.dma_start(out=w_sb[:, groups, :, :], in_=w_rows[:, groups, :, :])
+            nc.sync.dma_start(out=w_sb[:, j, :, :, :], in_=w_rows[:, j, :, :, :])
 
         def x_stats(m):
             squares = scratch.tile([P, D], BF16)
@@ -153,7 +152,7 @@ def tile_transformerblock_pa_kernel(tc, x, rms_w, w_qkv, out):
                 for r in range(GROUPS_PER_ROUND):
                     bank = psum_tr.tile([P, ROW_PAIR, HALVES, P], F32, tag="tr")
                     for a in range(ROW_PAIR):
-                        words = w_sb[:, GROUPS_PER_ROUND * j + r, a, :].bitcast(F32)
+                        words = w_sb[:, j, r, a, :].bitcast(F32)
                         for u in range(HALVES):
                             first = (HALVES * g + u) * P
                             nc.tensor.transpose(
@@ -169,7 +168,9 @@ def tile_transformerblock_pa_kernel(tc, x, rms_w, w_qkv, out):
                 0,
                 w_grouped[j][:]
                 .bitcast(F32)
-                .rearrange("p (b q a u) -> p b q a u", b=W_BANKS, a=ROW_PAIR, u=HALVES)[:, b],
+                .rearrange(
+                    "p (g q r a u) -> p g r q a u", g=PASSES, r=GROUPS_PER_ROUND, a=ROW_PAIR, u=HALVES
+                )[:, b // GROUPS_PER_ROUND, b % GROUPS_PER_ROUND],
                 w_banks[j][b][:].rearrange("p a u q -> p q a u"),
             )
 

from contextlib import ExitStack

import concourse.mybir as mybir
from concourse.masks import make_identity

F32 = mybir.dt.float32
BF16 = mybir.dt.bfloat16
U32 = mybir.dt.uint32
U8 = mybir.dt.uint8
FP8X4 = mybir.dt.float8_e4m3fn_x4
ACT = mybir.ActivationFunctionType
ALU = mybir.AluOpType

P = 128
S = 1024
D = 1024
N_OUT = 3072
EPS = 1e-5
PACK = 4
K_PASS = P * PACK
PASSES = D // K_PASS
HALVES = 2
S_TILES = S // P
N_ROUND = 512
ROUNDS = N_OUT // N_ROUND
HEAD = 128
HEADS_PER_ROUND = N_ROUND // HEAD
ROW_PAIR = 2
GROUP_ROWS = P * ROW_PAIR
GROUPS_PER_ROUND = N_ROUND // GROUP_ROWS
W_BANKS = PASSES * GROUPS_PER_ROUND
GROUP_TILES = 4

FLOPS = 2 * S * D * N_OUT


def tile_transformerblock_pa_kernel(tc, x, rms_w, w_qkv, out):
    nc = tc.nc
    x_rows = x.rearrange("b (p m) d -> p (b m) d", m=S_TILES)
    out_rows = out.rearrange("c b h (p m) f -> p (c b h) m f", m=S_TILES)
    w_rows = w_qkv.rearrange("(j q r a) d -> q j r a d", q=P, r=GROUPS_PER_ROUND, a=ROW_PAIR)

    with ExitStack() as ctx:
        keep = ctx.enter_context(tc.tile_pool(name="keep", bufs=1))
        scratch = ctx.enter_context(tc.tile_pool(name="scratch", bufs=2))
        x_group_pool = ctx.enter_context(tc.tile_pool(name="x_group", bufs=3))
        w_group_pool = ctx.enter_context(tc.tile_pool(name="w_group", bufs=2))
        stage_pool = ctx.enter_context(tc.tile_pool(name="stage", bufs=24 // GROUP_TILES))
        psum_tr = ctx.enter_context(tc.psum_pool(name="psum_tr", bufs=4))
        psum_acc = ctx.enter_context(tc.psum_pool(name="psum_acc", bufs=4))

        x_sb = keep.tile([P, S_TILES, D], BF16)
        xn = keep.tile([P, S_TILES, D], BF16)
        w_sb = keep.tile([P, ROUNDS, GROUPS_PER_ROUND, ROW_PAIR, D], BF16)
        gain_rows = keep.tile([P, D], BF16)
        gain_bc = keep.tile([P, D], BF16)
        ones = keep.tile([P, P], BF16)
        ident = keep.tile([P, P], F32)
        eps_col = keep.tile([P, 1], F32)
        warm = keep.tile([P, 1], F32)
        sum_sq = keep.tile([P, S_TILES], F32)
        rms = keep.tile([P, S_TILES], F32)
        inv_rms = keep.tile([P, S_TILES], F32)
        x_codes = keep.tile([P, S_TILES, PASSES * P], U32, align_bytes=64)
        x_scales = keep.tile([P, S_TILES, PASSES * P], U8, align_bytes=64)
        w_codes = keep.tile([P, ROUNDS, PASSES * N_ROUND], U32, align_bytes=64)
        w_scales = keep.tile([P, ROUNDS, PASSES * N_ROUND], U8, align_bytes=64)

        x_banks = {}
        x_grouped = {}
        w_banks = {}
        w_grouped = {}
        acc_banks = {}
        stages = {}

        def leave_psum(index, dst, src):
            if index % 2 == 0:
                nc.scalar.copy(out=dst, in_=src)
            else:
                nc.vector.tensor_copy(out=dst, in_=src)

        def load_x(first):
            tiles = slice(first, first + 2)
            nc.sync.dma_start(out=x_sb[:, tiles, :], in_=x_rows[:, tiles, :])

        def load_w(j):
            nc.sync.dma_start(out=w_sb[:, j, :, :, :], in_=w_rows[:, j, :, :, :])

        def x_stats(m):
            squares = scratch.tile([P, D], BF16)
            nc.scalar.activation(
                out=squares[:], in_=x_sb[:, m, :], func=ACT.Square, accum_out=sum_sq[:, m : m + 1]
            )
            nc.scalar.activation(
                out=rms[:, m : m + 1],
                in_=sum_sq[:, m : m + 1],
                func=ACT.Sqrt,
                bias=eps_col[:, 0:1],
                scale=1.0 / D,
            )

        def x_scale(m):
            nc.vector.reciprocal(out=inv_rms[:, m : m + 1], in_=rms[:, m : m + 1])
            nc.vector.scalar_tensor_tensor(
                out=xn[:, m, :],
                in0=x_sb[:, m, :],
                scalar=inv_rms[:, m : m + 1],
                in1=gain_bc[:],
                op0=ALU.mult,
                op1=ALU.mult,
            )

        def x_transpose(m):
            bank = psum_tr.tile([P, PASSES, HALVES, P], F32, tag="tr")
            words = xn[:, m, :].bitcast(F32)
            for g in range(PASSES):
                for u in range(HALVES):
                    first = (HALVES * g + u) * P
                    nc.tensor.transpose(bank[:, g, u, :], words[:, first : first + P], ident[:])
            x_banks[m] = bank

        def x_regroup(m):
            grouped = x_group_pool.tile([P, PASSES * P * PACK], BF16, align_bytes=64)
            nc.scalar.copy(
                out=grouped[:].bitcast(F32).rearrange("p (g s u) -> p g s u", g=PASSES, u=HALVES),
                in_=x_banks[m][:].rearrange("p g u s -> p g s u"),
            )
            x_grouped[m] = grouped

        def x_quantise(m):
            nc.vector.quantize_mx(
                out=x_codes[:, m, :].bitcast(FP8X4), scales=x_scales[:, m, :], in_=x_grouped[m][:]
            )

        def x_prepare(m):
            x_stats(m)
            x_scale(m)
            x_transpose(m)
            x_regroup(m)
            x_quantise(m)

        def w_prepare(j):
            w_transpose(j)
            for b in range(W_BANKS):
                w_regroup(j, b)
            for g in range(PASSES):
                w_quantise(j, g)

        def w_transpose(j):
            banks = []
            for g in range(PASSES):
                for r in range(GROUPS_PER_ROUND):
                    bank = psum_tr.tile([P, ROW_PAIR, HALVES, P], F32, tag="tr")
                    for a in range(ROW_PAIR):
                        words = w_sb[:, j, r, a, :].bitcast(F32)
                        for u in range(HALVES):
                            first = (HALVES * g + u) * P
                            nc.tensor.transpose(
                                bank[:, a, u, :], words[:, first : first + P], ident[:]
                            )
                    banks.append(bank)
            w_banks[j] = banks
            grouped = w_group_pool.tile([P, PASSES * N_ROUND * PACK], BF16, align_bytes=64)
            w_grouped[j] = grouped

        def w_regroup(j, b):
            leave_psum(
                0,
                w_grouped[j][:]
                .bitcast(F32)
                .rearrange(
                    "p (g q r a u) -> p g r q a u", g=PASSES, r=GROUPS_PER_ROUND, a=ROW_PAIR, u=HALVES
                )[:, b // GROUPS_PER_ROUND, b % GROUPS_PER_ROUND],
                w_banks[j][b][:].rearrange("p a u q -> p q a u"),
            )

        def w_quantise(j, g):
            cols = slice(g * N_ROUND, (g + 1) * N_ROUND)
            nc.vector.quantize_mx(
                out=w_codes[:, j, cols].bitcast(FP8X4),
                scales=w_scales[:, j, cols],
                in_=w_grouped[j][:, g * N_ROUND * PACK : (g + 1) * N_ROUND * PACK],
            )

        def product(j, m):
            acc = psum_acc.tile([P, N_ROUND], F32, tag="acc")
            for g in range(PASSES):
                nc.tensor.matmul_mx(
                    out=acc[:],
                    lhsT=x_codes[:, m, g * P : (g + 1) * P].bitcast(FP8X4),
                    lhsT_scale=x_scales[:, m, g * P : (g + 1) * P],
                    rhs=w_codes[:, j, g * N_ROUND : (g + 1) * N_ROUND].bitcast(FP8X4),
                    rhs_scale=w_scales[:, j, g * N_ROUND : (g + 1) * N_ROUND],
                    start=(g == 0),
                    stop=(g == PASSES - 1),
                )
            acc_banks[m] = acc

        def collect(j, m):
            if m % GROUP_TILES == 0:
                stage = stage_pool.tile([P, HEADS_PER_ROUND, GROUP_TILES, HEAD], F32)
                stages[0] = stage
            leave_psum(
                m if m >= GROUP_TILES else min(m, 1),
                stages[0][:, :, m % GROUP_TILES, :],
                acc_banks[m][:].rearrange("p (h f) -> p h f", h=HEADS_PER_ROUND),
            )
            if m % GROUP_TILES == GROUP_TILES - 1:
                nc.sync.dma_start(
                    out=out_rows[
                        :,
                        HEADS_PER_ROUND * j : HEADS_PER_ROUND * (j + 1),
                        m + 1 - GROUP_TILES : m + 1,
                        :,
                    ],
                    in_=stages[0][:],
                )

        nc.vector.memset(gain_rows[:], 0.0)
        nc.sync.dma_start(out=gain_rows[0:1, :], in_=rms_w.unsqueeze(0))
        load_x(0)
        load_x(2)
        load_w(0)
        load_x(4)
        load_x(6)
        for j in range(1, ROUNDS):
            load_w(j)

        nc.vector.memset(eps_col[:], EPS)
        nc.vector.memset(ones[:], 1.0)
        make_identity(nc, ident[:])
        nc.scalar.activation(out=warm[:], in_=eps_col[:], func=ACT.Sqrt)

        for half in range(D // N_ROUND):
            cols = slice(half * N_ROUND, (half + 1) * N_ROUND)
            spread = psum_tr.tile([P, N_ROUND], F32, tag="tr")
            nc.tensor.matmul(out=spread[:], lhsT=ones[:], rhs=gain_rows[:, cols], start=True, stop=True)
            nc.vector.tensor_copy(out=gain_bc[:, cols], in_=spread[:])

        x_prepare(0)
        x_prepare(1)
        w_prepare(0)
        for m in range(2, GROUP_TILES):
            x_prepare(m)

        for group in range(S_TILES // GROUP_TILES):
            for j in range(ROUNDS):
                if group == 0 and j + 1 < ROUNDS:
                    w_prepare(j + 1)
                for m in range(group * GROUP_TILES, (group + 1) * GROUP_TILES):
                    product(j, m)
                    collect(j, m)
                if j < GROUP_TILES and group + 1 < S_TILES // GROUP_TILES:
                    x_prepare((group + 1) * GROUP_TILES + j)
